import numpy as np
import ml_dtypes


def mxq(x, axis, fmt="e4m3"):
    dtype, down = {"e4m3": (ml_dtypes.float8_e4m3fn, 7), "e5m2": (ml_dtypes.float8_e5m2, 14)}[fmt]
    v = np.moveaxis(np.asarray(x, np.float32).astype(ml_dtypes.bfloat16).astype(np.float64), axis, -1)
    blocks = v.reshape(v.shape[:-1] + (-1, 32))
    amax = np.abs(blocks).max(-1, keepdims=True)
    byte = np.maximum(np.where(amax > 0, np.frexp(amax)[1] - 1 + 127, 0) - down, 1)
    scale = np.exp2(byte - 127.0)
    codes = (blocks / scale).astype(np.float32).astype(dtype).astype(np.float64)
    return np.moveaxis((codes * scale).reshape(v.shape), -1, axis)


WIDE = False


def mx_kscale(k):
    if not WIDE:
        return np.ones(k)
    levels = np.array([10, -10, 5, -5, 0])
    a = np.random.permutation(np.resize(levels, k // 512 * 4)).reshape(k // 512, 4)
    idx = np.arange(k)
    return np.exp2(a[idx // 512, idx % 128 // 32])


BF16 = ml_dtypes.bfloat16


def bf(x):
    return np.asarray(x, np.float32).astype(BF16)


def f64(x):
    return np.asarray(x).astype(np.float64)


B, S, C, MID = 4, 128, 256, 512
K0 = 2 * C


def gelu_tanh(v):
    return 0.5 * v * (1.0 + np.tanh(np.sqrt(2.0 / np.pi) * (v + 0.044715 * v**3)))


def setup_inputs():
    u = mx_kscale(K0)[:C]
    uu = np.concatenate([u, u])
    return {"sample_features": bf(np.random.standard_normal((B, S, C)) * u),
            "query_samples": bf(np.random.standard_normal((B, S, C)) * u),
            "pos_enc": bf(np.random.standard_normal((B, S, C)) * u),
            "W0": bf(np.random.standard_normal((K0, MID)) * 0.6 / np.sqrt(K0) / uu[:, None]),
            "b0": bf(np.random.standard_normal(MID) * 0.2),
            "W1": bf(np.random.standard_normal((MID, MID)) * 1.5 / np.sqrt(MID)),
            "b1": bf(np.random.standard_normal(MID) * 0.2)}


def reference(sample_features, query_samples, pos_enc, W0, b0, W1, b1):
    sf = f64(sample_features)
    q = f64(query_samples) + f64(pos_enc)
    x = np.concatenate([sf - q, q], axis=-1)
    h = gelu_tanh((mxq(x, 2, "e4m3") @ mxq(f64(W0), 0, "e4m3")) + f64(b0))
    return gelu_tanh((mxq(h, 2, "e4m3") @ mxq(f64(W1), 0, "e4m3")) + f64(b1))

@@ -1,0 +1,203 @@
+from contextlib import ExitStack
+
+import concourse.mybir as mybir
+from concourse.masks import make_identity
+
+BF16 = mybir.dt.bfloat16
+F32 = mybir.dt.float32
+U32 = mybir.dt.uint32
+U8 = mybir.dt.uint8
+FP8X4 = mybir.dt.float8_e4m3fn_x4
+GELU = mybir.ActivationFunctionType.Gelu_apprx_tanh
+ADD = mybir.AluOpType.add
+SUBTRACT = mybir.AluOpType.subtract
+
+P = 128
+PACK = 4
+TOKENS = 512
+C = 256
+K0 = 2 * C
+MID = 512
+GROUPS = TOKENS // P
+HALVES = 2
+HALF_GROUPS = GROUPS // HALVES
+HALF_TOKENS = TOKENS // HALVES
+RUN = 4
+
+FLOPS = 2 * TOKENS * K0 * MID + 2 * TOKENS * MID * MID
+
+
+def regroup(engine_copy, grouped, rows):
+    engine_copy(
+        out=grouped.rearrange("p (c i) j -> p c j i", i=RUN),
+        in_=rows.rearrange("p j (c i) -> p c j i", i=RUN),
+    )
+
+
+def tile_samplequerymessagepassing_pa_s_kernel(
+    tc, sample_features, query_samples, pos_enc, W0, b0, W1, b1, out
+):
+    nc = tc.nc
+    halves = range(HALVES)
+
+    def by_group(dram):
+        return dram.flatten_outer_dims().rearrange("(r g) c -> r g c", g=GROUPS)
+
+    with ExitStack() as ctx:
+        keep = ctx.enter_context(tc.tile_pool(name="keep", bufs=1))
+        psum = ctx.enter_context(tc.psum_pool(name="psum", bufs=8))
+
+        b1_row = keep.tile([P, MID], BF16)
+        nc.gpsimd.memset(b1_row[:], 0.0)
+        nc.scalar.dma_start(out=b1_row[0:1, :], in_=b1.rearrange("(o n) -> o n", o=1))
+        b0_bf = keep.tile([P, PACK], BF16)
+        nc.scalar.dma_start(out=b0_bf[:], in_=b0.rearrange("(q u) -> q u", u=PACK))
+
+        inputs = {}
+        for half in halves:
+            groups = slice(half * HALF_GROUPS, (half + 1) * HALF_GROUPS)
+            for name, dram in (("qs", query_samples), ("pe", pos_enc), ("sf", sample_features)):
+                loaded = keep.tile([P, HALF_GROUPS, C], BF16, name="%s%d" % (name, half))
+                nc.sync.dma_start(out=loaded[:], in_=by_group(dram)[:, groups, :])
+                inputs[(name, half)] = loaded
+        w0_rows = keep.tile([P, PACK, MID], BF16)
+        nc.sync.dma_start(out=w0_rows[:], in_=W0.rearrange("(t p) n -> p t n", p=P))
+        w1_rows = keep.tile([P, PACK, MID], BF16)
+        nc.sync.dma_start(out=w1_rows[:], in_=W1.rearrange("(q u) n -> q u n", u=PACK))
+
+        warm = keep.tile([P, 1], F32)
+        nc.vector.memset(warm[:], 0.0)
+        warmed = keep.tile([P, 1], F32)
+        nc.scalar.activation(out=warmed[:], in_=warm[:], func=GELU)
+
+        ident = keep.tile([P, P], BF16)
+        make_identity(nc, ident[:])
+        ones = keep.tile([P, P], BF16)
+        nc.gpsimd.memset(ones[:], 1.0)
+
+        b0_f32 = keep.tile([P, PACK], F32)
+        nc.gpsimd.tensor_copy(out=b0_f32[:], in_=b0_bf[:])
+
+        b1_ps = psum.tile([P, MID], F32, tag="bank")
+        nc.tensor.matmul(out=b1_ps[:], lhsT=ones[:], rhs=b1_row[:], start=True, stop=True)
+        b1_all = keep.tile([P, MID], F32)
+        nc.scalar.copy(out=b1_all[:], in_=b1_ps[:])
+
+        q_f32 = []
+        x_bf = []
+        for half in halves:
+            q = keep.tile([P, HALF_GROUPS, C], F32, name="q_f32_%d" % half)
+            nc.vector.tensor_tensor(
+                out=q[:], in0=inputs[("qs", half)][:], in1=inputs[("pe", half)][:], op=ADD
+            )
+            q_f32.append(q)
+            x_bf.append(keep.tile([P, HALF_GROUPS, K0], BF16, name="x_bf%d" % half))
+        for half in halves:
+            nc.scalar.copy(out=x_bf[half][:, :, C:K0], in_=q_f32[half][:])
+        for half in halves:
+            nc.vector.tensor_tensor(
+                out=x_bf[half][:, :, 0:C], in0=inputs[("sf", half)][:], in1=q_f32[half][:], op=SUBTRACT
+            )
+
+        x_grouped = []
+        for half in halves:
+            grouped = keep.tile([P, HALF_GROUPS, P, PACK], BF16, name="x_grouped%d" % half, align_bytes=64)
+            for i in range(HALF_GROUPS):
+                xt = psum.tile([P, PACK, P], BF16, tag="bank")
+                for t in range(PACK):
+                    nc.tensor.transpose(xt[:, t, :], x_bf[half][:, i, t * P : (t + 1) * P], ident[:])
+                nc.scalar.copy(out=grouped[:, i, :, :], in_=xt[:].rearrange("p t r -> p r t"))
+            x_grouped.append(grouped)
+
+        w0_grouped = keep.tile([P, PACK, P, PACK], BF16, align_bytes=64)
+        w0_codes = keep.tile([P, MID], U32, align_bytes=64)
+        w0_scales = keep.tile([P, MID], U8, align_bytes=64)
+        nc.vector.tensor_copy(
+            out=w0_grouped[:].rearrange("p u q t -> p q t u"),
+            in_=w0_rows[:].rearrange("p t (q u) -> p q t u", u=PACK),
+        )
+
+        x_codes = []
+        x_scales = []
+        for half in halves:
+            x_codes.append(keep.tile([P, HALF_TOKENS], U32, name="x_codes%d" % half, align_bytes=64))
+            x_scales.append(keep.tile([P, HALF_TOKENS], U8, name="x_scales%d" % half, align_bytes=64))
+
+        def quantise_x(half):
+            nc.vector.quantize_mx(
+                out=x_codes[half][:].bitcast(FP8X4),
+                scales=x_scales[half][:],
+                in_=x_grouped[half][:].rearrange("p g r t -> p (g r t)"),
+            )
+
+        quantise_x(0)
+        nc.vector.quantize_mx(
+            out=w0_codes[:].bitcast(FP8X4),
+            scales=w0_scales[:],
+            in_=w0_grouped[:].rearrange("p u q t -> p (u q t)"),
+        )
+        quantise_x(1)
+
+        w1_grouped = keep.tile([P, MID, PACK], BF16, align_bytes=64)
+        w1_codes = keep.tile([P, MID], U32, align_bytes=64)
+        w1_scales = keep.tile([P, MID], U8, align_bytes=64)
+        for half in halves:
+            cols = slice(half * (MID // 2), (half + 1) * (MID // 2))
+            regroup(nc.vector.tensor_copy, w1_grouped[:, cols, :], w1_rows[:, :, cols])
+        for half in halves:
+            cols = slice(half * (MID // 2), (half + 1) * (MID // 2))
+            nc.vector.quantize_mx(
+                out=w1_codes[:, cols].bitcast(FP8X4),
+                scales=w1_scales[:, cols],
+                in_=w1_grouped[:, cols, :].rearrange("p c j -> p (c j)"),
+            )
+
+        h_codes = []
+        h_scales = []
+        for half in halves:
+            h_bf = keep.tile([P, PACK, HALF_TOKENS], BF16, name="h_bf%d" % half)
+            for pair in range(PACK // 2):
+                h_ps = psum.tile([P, 2, HALF_TOKENS], F32, tag="bank")
+                for i in range(2):
+                    u = 2 * pair + i
+                    nc.tensor.matmul_mx(
+                        out=h_ps[:, i, :],
+                        lhsT=w0_codes[:, u * P : (u + 1) * P].bitcast(FP8X4),
+                        lhsT_scale=w0_scales[:, u * P : (u + 1) * P],
+                        rhs=x_codes[half][:].bitcast(FP8X4),
+                        rhs_scale=x_scales[half][:],
+                        start=True,
+                        stop=True,
+                    )
+                for i in range(2):
+                    u = 2 * pair + i
+                    nc.scalar.activation(
+                        out=h_bf[:, u, :], in_=h_ps[:, i, :], func=GELU, bias=b0_f32[:, u : u + 1], scale=1.0
+                    )
+            h_grouped = keep.tile([P, HALF_TOKENS, PACK], BF16, name="h_grouped%d" % half, align_bytes=64)
+            regroup(nc.vector.tensor_copy, h_grouped[:], h_bf[:])
+            codes = keep.tile([P, HALF_TOKENS], U32, name="h_codes%d" % half, align_bytes=64)
+            scales = keep.tile([P, HALF_TOKENS], U8, name="h_scales%d" % half, align_bytes=64)
+            nc.vector.quantize_mx(
+                out=codes[:].bitcast(FP8X4), scales=scales[:], in_=h_grouped[:].rearrange("p c u -> p (c u)")
+            )
+            h_codes.append(codes)
+            h_scales.append(scales)
+
+        for g in range(GROUPS):
+            half, i = divmod(g, HALF_GROUPS)
+            o_ps = psum.tile([P, MID], F32, tag="bank")
+            nc.tensor.matmul_mx(
+                out=o_ps[:],
+                lhsT=h_codes[half][:, i * P : (i + 1) * P].bitcast(FP8X4),
+                lhsT_scale=h_scales[half][:, i * P : (i + 1) * P],
+                rhs=w1_codes[:].bitcast(FP8X4),
+                rhs_scale=w1_scales[:],
+                start=True,
+                stop=True,
+            )
+            biased = keep.tile([P, MID], F32, name="biased%d" % g)
+            nc.vector.tensor_tensor(out=biased[:], in0=o_ps[:], in1=b1_all[:], op=ADD)
+            result = keep.tile([P, MID], F32, name="result%d" % g)
+            nc.scalar.activation(out=result[:], in_=biased[:], func=GELU)
+            nc.sync.dma_start(out=by_group(out)[:, g, :], in_=result[:])

@@ -21,27 +21,43 @@ MID = 512
 GROUPS = TOKENS // P
 HALVES = 2
 HALF_GROUPS = GROUPS // HALVES
-HALF_TOKENS = TOKENS // HALVES
+HALF = TOKENS // HALVES
 RUN = 4
 
 FLOPS = 2 * TOKENS * K0 * MID + 2 * TOKENS * MID * MID
 
 
-def regroup(engine_copy, grouped, rows):
-    engine_copy(
-        out=grouped.rearrange("p (c i) j -> p c j i", i=RUN),
-        in_=rows.rearrange("p j (c i) -> p c j i", i=RUN),
-    )
+def half_of(index):
+    return slice(index * HALF, (index + 1) * HALF)
 
 
 def tile_samplequerymessagepassing_pa_s_kernel(
     tc, sample_features, query_samples, pos_enc, W0, b0, W1, b1, out
 ):
     nc = tc.nc
-    halves = range(HALVES)
 
     def by_group(dram):
         return dram.flatten_outer_dims().rearrange("(r g) c -> r g c", g=GROUPS)
+
+    def regroup(grouped, rows):
+        nc.vector.tensor_copy(
+            out=grouped.rearrange("p (c i) j -> p c j i", i=RUN),
+            in_=rows.rearrange("p j (c i) -> p c j i", i=RUN),
+        )
+
+    def quantise(codes, scales, grouped):
+        nc.vector.quantize_mx(out=codes.bitcast(FP8X4), scales=scales, in_=grouped)
+
+    def mx_pass(acc, stationary, moving):
+        nc.tensor.matmul_mx(
+            out=acc,
+            lhsT=stationary[0].bitcast(FP8X4),
+            lhsT_scale=stationary[1],
+            rhs=moving[0].bitcast(FP8X4),
+            rhs_scale=moving[1],
+            start=True,
+            stop=True,
+        )
 
     with ExitStack() as ctx:
         keep = ctx.enter_context(tc.tile_pool(name="keep", bufs=1))
@@ -53,13 +69,12 @@ def tile_samplequerymessagepassing_pa_s_kernel(
         b0_bf = keep.tile([P, PACK], BF16)
         nc.scalar.dma_start(out=b0_bf[:], in_=b0.rearrange("(q u) -> q u", u=PACK))
 
-        inputs = {}
-        for half in halves:
+        loaded = {}
+        for half in range(HALVES):
             groups = slice(half * HALF_GROUPS, (half + 1) * HALF_GROUPS)
             for name, dram in (("qs", query_samples), ("pe", pos_enc), ("sf", sample_features)):
-                loaded = keep.tile([P, HALF_GROUPS, C], BF16, name="%s%d" % (name, half))
-                nc.sync.dma_start(out=loaded[:], in_=by_group(dram)[:, groups, :])
-                inputs[(name, half)] = loaded
+                loaded[(name, half)] = keep.tile([P, HALF_GROUPS, C], BF16, name="%s%d" % (name, half))
+                nc.sync.dma_start(out=loaded[(name, half)][:], in_=by_group(dram)[:, groups, :])
         w0_rows = keep.tile([P, PACK, MID], BF16)
         nc.sync.dma_start(out=w0_rows[:], in_=W0.rearrange("(t p) n -> p t n", p=P))
         w1_rows = keep.tile([P, PACK, MID], BF16)
@@ -70,7 +85,7 @@ def tile_samplequerymessagepassing_pa_s_kernel(
         warmed = keep.tile([P, 1], F32)
         nc.scalar.activation(out=warmed[:], in_=warm[:], func=GELU)
 
-        ident = keep.tile([P, P], BF16)
+        ident = keep.tile([P, P], F32)
         make_identity(nc, ident[:])
         ones = keep.tile([P, P], BF16)
         nc.gpsimd.memset(ones[:], 1.0)
@@ -83,121 +98,101 @@ def tile_samplequerymessagepassing_pa_s_kernel(
         b1_all = keep.tile([P, MID], F32)
         nc.scalar.copy(out=b1_all[:], in_=b1_ps[:])
 
-        q_f32 = []
-        x_bf = []
-        for half in halves:
-            q = keep.tile([P, HALF_GROUPS, C], F32, name="q_f32_%d" % half)
-            nc.vector.tensor_tensor(
-                out=q[:], in0=inputs[("qs", half)][:], in1=inputs[("pe", half)][:], op=ADD
-            )
-            q_f32.append(q)
-            x_bf.append(keep.tile([P, HALF_GROUPS, K0], BF16, name="x_bf%d" % half))
-        for half in halves:
-            nc.scalar.copy(out=x_bf[half][:, :, C:K0], in_=q_f32[half][:])
-        for half in halves:
-            nc.vector.tensor_tensor(
-                out=x_bf[half][:, :, 0:C], in0=inputs[("sf", half)][:], in1=q_f32[half][:], op=SUBTRACT
-            )
-
         x_grouped = []
-        for half in halves:
+        for half in range(HALVES):
+            x_f32 = keep.tile([P, HALF_GROUPS, K0], F32, name="x_f32_%d" % half)
+            q_part = x_f32[:, :, C:K0]
+            nc.vector.tensor_tensor(out=q_part, in0=loaded[("qs", half)][:], in1=loaded[("pe", half)][:], op=ADD)
+            nc.vector.tensor_tensor(out=x_f32[:, :, 0:C], in0=loaded[("sf", half)][:], in1=q_part, op=SUBTRACT)
             grouped = keep.tile([P, HALF_GROUPS, P, PACK], BF16, name="x_grouped%d" % half, align_bytes=64)
             for i in range(HALF_GROUPS):
-                xt = psum.tile([P, PACK, P], BF16, tag="bank")
+                xt = psum.tile([P, PACK, P], F32, tag="bank")
                 for t in range(PACK):
-                    nc.tensor.transpose(xt[:, t, :], x_bf[half][:, i, t * P : (t + 1) * P], ident[:])
+                    nc.tensor.transpose(xt[:, t, :], x_f32[:, i, t * P : (t + 1) * P], ident[:])
                 nc.scalar.copy(out=grouped[:, i, :, :], in_=xt[:].rearrange("p t r -> p r t"))
             x_grouped.append(grouped)
 
         w0_grouped = keep.tile([P, PACK, P, PACK], BF16, align_bytes=64)
         w0_codes = keep.tile([P, MID], U32, align_bytes=64)
         w0_scales = keep.tile([P, MID], U8, align_bytes=64)
-        nc.vector.tensor_copy(
-            out=w0_grouped[:].rearrange("p u q t -> p q t u"),
-            in_=w0_rows[:].rearrange("p t (q u) -> p q t u", u=PACK),
-        )
-
-        x_codes = []
-        x_scales = []
-        for half in halves:
-            x_codes.append(keep.tile([P, HALF_TOKENS], U32, name="x_codes%d" % half, align_bytes=64))
-            x_scales.append(keep.tile([P, HALF_TOKENS], U8, name="x_scales%d" % half, align_bytes=64))
-
-        def quantise_x(half):
-            nc.vector.quantize_mx(
-                out=x_codes[half][:].bitcast(FP8X4),
-                scales=x_scales[half][:],
-                in_=x_grouped[half][:].rearrange("p g r t -> p (g r t)"),
+        x_codes = keep.tile([P, TOKENS], U32, align_bytes=64)
+        x_scales = keep.tile([P, TOKENS], U8, align_bytes=64)
+        w0_sorted = w0_rows[:].rearrange("p t (q u) -> p q t u", u=PACK)
+        for half in range(HALVES):
+            passes = slice(half * 2, half * 2 + 2)
+            nc.vector.tensor_copy(
+                out=w0_grouped[:, passes, :, :].rearrange("p u q t -> p q t u"), in_=w0_sorted[:, :, :, passes]
+            )
+            quantise(
+                x_codes[:, half_of(half)],
+                x_scales[:, half_of(half)],
+                x_grouped[half][:].rearrange("p g r t -> p (g r t)"),
+            )
+            quantise(
+                w0_codes[:, half_of(half)],
+                w0_scales[:, half_of(half)],
+                w0_grouped[:, passes, :, :].rearrange("p u q t -> p (u q t)"),
             )
 
-        quantise_x(0)
-        nc.vector.quantize_mx(
-            out=w0_codes[:].bitcast(FP8X4),
-            scales=w0_scales[:],
-            in_=w0_grouped[:].rearrange("p u q t -> p (u q t)"),
-        )
-        quantise_x(1)
-
-        w1_grouped = keep.tile([P, MID, PACK], BF16, align_bytes=64)
-        w1_codes = keep.tile([P, MID], U32, align_bytes=64)
-        w1_scales = keep.tile([P, MID], U8, align_bytes=64)
-        for half in halves:
-            cols = slice(half * (MID // 2), (half + 1) * (MID // 2))
-            regroup(nc.vector.tensor_copy, w1_grouped[:, cols, :], w1_rows[:, :, cols])
-        for half in halves:
-            cols = slice(half * (MID // 2), (half + 1) * (MID // 2))
-            nc.vector.quantize_mx(
-                out=w1_codes[:, cols].bitcast(FP8X4),
-                scales=w1_scales[:, cols],
-                in_=w1_grouped[:, cols, :].rearrange("p c j -> p (c j)"),
-            )
-
-        h_codes = []
-        h_scales = []
-        for half in halves:
-            h_bf = keep.tile([P, PACK, HALF_TOKENS], BF16, name="h_bf%d" % half)
+        h_bf = []
+        for half in range(HALVES):
+            h_bf.append(keep.tile([P, PACK, HALF], BF16, name="h_bf%d" % half))
             for pair in range(PACK // 2):
-                h_ps = psum.tile([P, 2, HALF_TOKENS], F32, tag="bank")
+                h_ps = psum.tile([P, 2, HALF], F32, tag="bank")
                 for i in range(2):
                     u = 2 * pair + i
-                    nc.tensor.matmul_mx(
-                        out=h_ps[:, i, :],
-                        lhsT=w0_codes[:, u * P : (u + 1) * P].bitcast(FP8X4),
-                        lhsT_scale=w0_scales[:, u * P : (u + 1) * P],
-                        rhs=x_codes[half][:].bitcast(FP8X4),
-                        rhs_scale=x_scales[half][:],
-                        start=True,
-                        stop=True,
+                    cols = slice(u * P, (u + 1) * P)
+                    mx_pass(
+                        h_ps[:, i, :],
+                        (w0_codes[:, cols], w0_scales[:, cols]),
+                        (x_codes[:, half_of(half)], x_scales[:, half_of(half)]),
                     )
                 for i in range(2):
                     u = 2 * pair + i
                     nc.scalar.activation(
-                        out=h_bf[:, u, :], in_=h_ps[:, i, :], func=GELU, bias=b0_f32[:, u : u + 1], scale=1.0
+                        out=h_bf[half][:, u, :], in_=h_ps[:, i, :], func=GELU, bias=b0_f32[:, u : u + 1], scale=1.0
                     )
-            h_grouped = keep.tile([P, HALF_TOKENS, PACK], BF16, name="h_grouped%d" % half, align_bytes=64)
-            regroup(nc.vector.tensor_copy, h_grouped[:], h_bf[:])
-            codes = keep.tile([P, HALF_TOKENS], U32, name="h_codes%d" % half, align_bytes=64)
-            scales = keep.tile([P, HALF_TOKENS], U8, name="h_scales%d" % half, align_bytes=64)
-            nc.vector.quantize_mx(
-                out=codes[:].bitcast(FP8X4), scales=scales[:], in_=h_grouped[:].rearrange("p c u -> p (c u)")
-            )
-            h_codes.append(codes)
-            h_scales.append(scales)
 
-        for g in range(GROUPS):
-            half, i = divmod(g, HALF_GROUPS)
-            o_ps = psum.tile([P, MID], F32, tag="bank")
-            nc.tensor.matmul_mx(
-                out=o_ps[:],
-                lhsT=h_codes[half][:, i * P : (i + 1) * P].bitcast(FP8X4),
-                lhsT_scale=h_scales[half][:, i * P : (i + 1) * P],
-                rhs=w1_codes[:].bitcast(FP8X4),
-                rhs_scale=w1_scales[:],
-                start=True,
-                stop=True,
+        w1_grouped = keep.tile([P, MID, PACK], BF16, align_bytes=64)
+        w1_codes = keep.tile([P, MID], U32, align_bytes=64)
+        w1_scales = keep.tile([P, MID], U8, align_bytes=64)
+        h_grouped = keep.tile([P, TOKENS, PACK], BF16, align_bytes=64)
+        h_codes = keep.tile([P, TOKENS], U32, align_bytes=64)
+        h_scales = keep.tile([P, TOKENS], U8, align_bytes=64)
+
+        def quantise_w1(half):
+            quantise(
+                w1_codes[:, half_of(half)],
+                w1_scales[:, half_of(half)],
+                w1_grouped[:, half_of(half), :].rearrange("p c j -> p (c j)"),
             )
+
+        def quantise_h(half):
+            quantise(
+                h_codes[:, half_of(half)],
+                h_scales[:, half_of(half)],
+                h_grouped[:, half_of(half), :].rearrange("p c u -> p (c u)"),
+            )
+
+        def layer2(g):
+            cols = slice(g * P, (g + 1) * P)
+            o_ps = psum.tile([P, MID], F32, tag="bank")
+            mx_pass(o_ps[:], (h_codes[:, cols], h_scales[:, cols]), (w1_codes[:], w1_scales[:]))
             biased = keep.tile([P, MID], F32, name="biased%d" % g)
             nc.vector.tensor_tensor(out=biased[:], in0=o_ps[:], in1=b1_all[:], op=ADD)
             result = keep.tile([P, MID], F32, name="result%d" % g)
             nc.scalar.activation(out=result[:], in_=biased[:], func=GELU)
             nc.sync.dma_start(out=by_group(out)[:, g, :], in_=result[:])
+
+        regroup(w1_grouped[:, half_of(0), :], w1_rows[:, :, half_of(0)])
+        regroup(w1_grouped[:, half_of(1), :], w1_rows[:, :, half_of(1)])
+        quantise_w1(0)
+        regroup(h_grouped[:, half_of(0), :], h_bf[0][:])
+        quantise_w1(1)
+        quantise_h(0)
+        regroup(h_grouped[:, half_of(1), :], h_bf[1][:])
+        layer2(0)
+        quantise_h(1)
+        layer2(1)
+        layer2(2)
+        layer2(3)

@@ -62,6 +62,7 @@ def tile_samplequerymessagepassing_pa_s_kernel(
     with ExitStack() as ctx:
         keep = ctx.enter_context(tc.tile_pool(name="keep", bufs=1))
         psum = ctx.enter_context(tc.psum_pool(name="psum", bufs=8))
+        ctx.enter_context(tc.manual_schedule())
 
         b1_row = keep.tile([P, MID], BF16)
         nc.gpsimd.memset(b1_row[:], 0.0)

@@ -64,20 +64,23 @@ def tile_samplequerymessagepassing_pa_s_kernel(
         psum = ctx.enter_context(tc.psum_pool(name="psum", bufs=8))
         ctx.enter_context(tc.manual_schedule())
 
-        b1_row = keep.tile([P, MID], BF16)
-        nc.gpsimd.memset(b1_row[:], 0.0)
-        nc.scalar.dma_start(out=b1_row[0:1, :], in_=b1.rearrange("(o n) -> o n", o=1))
-        b0_bf = keep.tile([P, PACK], BF16)
-        nc.scalar.dma_start(out=b0_bf[:], in_=b0.rearrange("(q u) -> q u", u=PACK))
-
         loaded = {}
         for half in range(HALVES):
             groups = slice(half * HALF_GROUPS, (half + 1) * HALF_GROUPS)
-            for name, dram in (("qs", query_samples), ("pe", pos_enc), ("sf", sample_features)):
+            for name, dram in (("qs", query_samples), ("pe", pos_enc)):
                 loaded[(name, half)] = keep.tile([P, HALF_GROUPS, C], BF16, name="%s%d" % (name, half))
                 nc.sync.dma_start(out=loaded[(name, half)][:], in_=by_group(dram)[:, groups, :])
+        sf_all = keep.tile([P, GROUPS, C], BF16)
+        nc.sync.dma_start(out=sf_all[:], in_=by_group(sample_features))
         w0_rows = keep.tile([P, PACK, MID], BF16)
-        nc.sync.dma_start(out=w0_rows[:], in_=W0.rearrange("(t p) n -> p t n", p=P))
+        nc.sync.dma_start(
+            out=w0_rows[:].rearrange("p (v e) n -> p v e n", e=2), in_=W0.rearrange("(v p e) n -> p v e n", p=P, e=2)
+        )
+        b0_bf = keep.tile([P, PACK], BF16)
+        nc.sync.dma_start(out=b0_bf[:], in_=b0.rearrange("(q u) -> q u", u=PACK))
+        b1_row = keep.tile([P, MID], BF16)
+        nc.gpsimd.memset(b1_row[:], 0.0)
+        nc.sync.dma_start(out=b1_row[0:1, :], in_=b1.rearrange("(o n) -> o n", o=1))
         w1_rows = keep.tile([P, PACK, MID], BF16)
         nc.sync.dma_start(out=w1_rows[:], in_=W1.rearrange("(q u) n -> q u n", u=PACK))
 
@@ -91,27 +94,42 @@ def tile_samplequerymessagepassing_pa_s_kernel(
         ones = keep.tile([P, P], BF16)
         nc.gpsimd.memset(ones[:], 1.0)
 
-        b0_f32 = keep.tile([P, PACK], F32)
-        nc.gpsimd.tensor_copy(out=b0_f32[:], in_=b0_bf[:])
-
-        b1_ps = psum.tile([P, MID], F32, tag="bank")
-        nc.tensor.matmul(out=b1_ps[:], lhsT=ones[:], rhs=b1_row[:], start=True, stop=True)
-        b1_all = keep.tile([P, MID], F32)
-        nc.scalar.copy(out=b1_all[:], in_=b1_ps[:])
-
+        q_f32 = []
+        x_bf = []
         x_grouped = []
+        xt = []
         for half in range(HALVES):
-            x_f32 = keep.tile([P, HALF_GROUPS, K0], F32, name="x_f32_%d" % half)
-            q_part = x_f32[:, :, C:K0]
-            nc.vector.tensor_tensor(out=q_part, in0=loaded[("qs", half)][:], in1=loaded[("pe", half)][:], op=ADD)
-            nc.vector.tensor_tensor(out=x_f32[:, :, 0:C], in0=loaded[("sf", half)][:], in1=q_part, op=SUBTRACT)
-            grouped = keep.tile([P, HALF_GROUPS, P, PACK], BF16, name="x_grouped%d" % half, align_bytes=64)
+            q_f32.append(keep.tile([P, HALF_GROUPS, C], F32, name="q_f32_%d" % half))
+            x_bf.append(keep.tile([P, HALF_GROUPS, K0], BF16, name="x_bf_%d" % half))
+            x_grouped.append(keep.tile([P, HALF_GROUPS, P, PACK], BF16, name="x_grouped%d" % half, align_bytes=64))
+            xt.append(psum.tile([P, HALF_GROUPS, 2, P], F32, tag="bank", name="xt%d" % half))
+
+        def transpose_words(half, v):
+            words = x_bf[half][:].rearrange("p g c -> p (g c)").bitcast(F32)
             for i in range(HALF_GROUPS):
-                xt = psum.tile([P, PACK, P], F32, tag="bank")
-                for t in range(PACK):
-                    nc.tensor.transpose(xt[:, t, :], x_f32[:, i, t * P : (t + 1) * P], ident[:])
-                nc.scalar.copy(out=grouped[:, i, :, :], in_=xt[:].rearrange("p t r -> p r t"))
-            x_grouped.append(grouped)
+                first = i * C + v * P
+                nc.tensor.transpose(xt[half][:, i, v, :], words[:, first : first + P], ident[:])
+
+        for half in range(HALVES):
+            nc.vector.tensor_tensor(
+                out=q_f32[half][:], in0=loaded[("qs", half)][:], in1=loaded[("pe", half)][:], op=ADD
+            )
+            nc.scalar.copy(out=x_bf[half][:, :, C:K0], in_=q_f32[half][:])
+            transpose_words(half, 1)
+        for half in range(HALVES):
+            nc.vector.tensor_tensor(
+                out=x_bf[half][:, :, 0:C], in0=sf_all[:, half * HALF_GROUPS : (half + 1) * HALF_GROUPS, :], in1=q_f32[half][:], op=SUBTRACT
+            )
+            transpose_words(half, 0)
+
+        def empty_words(half):
+            nc.scalar.copy(
+                out=x_grouped[half][:]
+                .rearrange("p g r t -> p (g r t)")
+                .bitcast(F32)
+                .rearrange("p (g r v) -> p g r v", r=P, v=2),
+                in_=xt[half][:].rearrange("p g v r -> p g r v"),
+            )
 
         w0_grouped = keep.tile([P, PACK, P, PACK], BF16, align_bytes=64)
         w0_codes = keep.tile([P, MID], U32, align_bytes=64)
@@ -119,40 +137,20 @@ def tile_samplequerymessagepassing_pa_s_kernel(
         x_codes = keep.tile([P, TOKENS], U32, align_bytes=64)
         x_scales = keep.tile([P, TOKENS], U8, align_bytes=64)
         w0_sorted = w0_rows[:].rearrange("p t (q u) -> p q t u", u=PACK)
-        for half in range(HALVES):
-            passes = slice(half * 2, half * 2 + 2)
-            nc.vector.tensor_copy(
-                out=w0_grouped[:, passes, :, :].rearrange("p u q t -> p q t u"), in_=w0_sorted[:, :, :, passes]
-            )
+
+        def quantise_x(half):
             quantise(
                 x_codes[:, half_of(half)],
                 x_scales[:, half_of(half)],
                 x_grouped[half][:].rearrange("p g r t -> p (g r t)"),
             )
+
+        def quantise_w0(half):
             quantise(
                 w0_codes[:, half_of(half)],
                 w0_scales[:, half_of(half)],
-                w0_grouped[:, passes, :, :].rearrange("p u q t -> p (u q t)"),
+                w0_grouped[:, half * 2 : half * 2 + 2, :, :].rearrange("p u q t -> p (u q t)"),
             )
-
-        h_bf = []
-        for half in range(HALVES):
-            h_bf.append(keep.tile([P, PACK, HALF], BF16, name="h_bf%d" % half))
-            for pair in range(PACK // 2):
-                h_ps = psum.tile([P, 2, HALF], F32, tag="bank")
-                for i in range(2):
-                    u = 2 * pair + i
-                    cols = slice(u * P, (u + 1) * P)
-                    mx_pass(
-                        h_ps[:, i, :],
-                        (w0_codes[:, cols], w0_scales[:, cols]),
-                        (x_codes[:, half_of(half)], x_scales[:, half_of(half)]),
-                    )
-                for i in range(2):
-                    u = 2 * pair + i
-                    nc.scalar.activation(
-                        out=h_bf[half][:, u, :], in_=h_ps[:, i, :], func=GELU, bias=b0_f32[:, u : u + 1], scale=1.0
-                    )
 
         w1_grouped = keep.tile([P, MID, PACK], BF16, align_bytes=64)
         w1_codes = keep.tile([P, MID], U32, align_bytes=64)
@@ -175,6 +173,61 @@ def tile_samplequerymessagepassing_pa_s_kernel(
                 h_grouped[:, half_of(half), :].rearrange("p c u -> p (c u)"),
             )
 
+        nc.scalar.copy(out=w0_grouped[:, 3, :, :], in_=w0_sorted[:, :, :, 3])
+        empty_words(0)
+        empty_words(1)
+        nc.vector.tensor_copy(
+            out=w0_grouped[:, 0:2, :, :].rearrange("p u q t -> p q t u"), in_=w0_sorted[:, :, :, 0:2]
+        )
+        nc.vector.tensor_copy(out=w0_grouped[:, 2, :, :], in_=w0_sorted[:, :, :, 2])
+        regroup(w1_grouped[:, half_of(0), :], w1_rows[:, :, half_of(0)])
+        quantise_x(0)
+        quantise_w0(0)
+        quantise_w0(1)
+        quantise_x(1)
+        regroup(w1_grouped[:, half_of(1), :], w1_rows[:, :, half_of(1)])
+        quantise_w1(0)
+
+        spare = psum.tile([P, MID], F32, tag="bank")
+        for half in range(HALVES):
+            nc.tensor.matmul(
+                out=spare[:],
+                lhsT=ones[:],
+                rhs=sf_all[:, half * HALF_GROUPS : (half + 1) * HALF_GROUPS, :].rearrange("p g c -> p (g c)"),
+                start=True,
+                stop=True,
+            )
+
+        b1_ps = psum.tile([P, MID], F32, tag="bank")
+        nc.tensor.matmul(out=b1_ps[:], lhsT=ones[:], rhs=b1_row[:], start=True, stop=True)
+        b1_all = keep.tile([P, MID], F32)
+
+        h_bf = []
+        for half in range(HALVES):
+            h_bf.append(keep.tile([P, PACK, HALF], BF16, name="h_bf%d" % half))
+
+        def layer1(half, pair):
+            h_ps = psum.tile([P, 2, HALF], F32, tag="bank", name="h_ps%d%d" % (half, pair))
+            for i in range(2):
+                u = 2 * pair + i
+                cols = slice(u * P, (u + 1) * P)
+                mx_pass(
+                    h_ps[:, i, :],
+                    (w0_codes[:, cols], w0_scales[:, cols]),
+                    (x_codes[:, half_of(half)], x_scales[:, half_of(half)]),
+                )
+            for i in range(2):
+                u = 2 * pair + i
+                nc.scalar.activation(
+                    out=h_bf[half][:, u, :], in_=h_ps[:, i, :], func=GELU, bias=b0_bf[:, u : u + 1], scale=1.0
+                )
+
+        layer1(0, 0)
+        layer1(0, 1)
+        layer1(1, 0)
+        layer1(1, 1)
+        nc.scalar.copy(out=b1_all[:], in_=b1_ps[:])
+
         def layer2(g):
             cols = slice(g * P, (g + 1) * P)
             o_ps = psum.tile([P, MID], F32, tag="bank")
@@ -185,9 +238,6 @@ def tile_samplequerymessagepassing_pa_s_kernel(
             nc.scalar.activation(out=result[:], in_=biased[:], func=GELU)
             nc.sync.dma_start(out=by_group(out)[:, g, :], in_=result[:])
 
-        regroup(w1_grouped[:, half_of(0), :], w1_rows[:, :, half_of(0)])
-        regroup(w1_grouped[:, half_of(1), :], w1_rows[:, :, half_of(1)])
-        quantise_w1(0)
         regroup(h_grouped[:, half_of(0), :], h_bf[0][:])
         quantise_w1(1)
         quantise_h(0)

@@ -27,6 +27,10 @@ RUN = 4
 FLOPS = 2 * TOKENS * K0 * MID + 2 * TOKENS * MID * MID
 
 
+def group_of(index):
+    return slice(index * P, (index + 1) * P)
+
+
 def half_of(index):
     return slice(index * HALF, (index + 1) * HALF)
 
@@ -39,8 +43,8 @@ def tile_samplequerymessagepassing_pa_s_kernel(
     def by_group(dram):
         return dram.flatten_outer_dims().rearrange("(r g) c -> r g c", g=GROUPS)
 
-    def regroup(grouped, rows):
-        nc.vector.tensor_copy(
+    def regroup(grouped, rows, copy=nc.vector.tensor_copy):
+        copy(
             out=grouped.rearrange("p (c i) j -> p c j i", i=RUN),
             in_=rows.rearrange("p j (c i) -> p c j i", i=RUN),
         )
@@ -78,11 +82,10 @@ def tile_samplequerymessagepassing_pa_s_kernel(
         )
         b0_bf = keep.tile([P, PACK], BF16)
         nc.sync.dma_start(out=b0_bf[:], in_=b0.rearrange("(q u) -> q u", u=PACK))
-        b1_row = keep.tile([P, MID], BF16)
-        nc.gpsimd.memset(b1_row[:], 0.0)
-        nc.sync.dma_start(out=b1_row[0:1, :], in_=b1.rearrange("(o n) -> o n", o=1))
         w1_rows = keep.tile([P, PACK, MID], BF16)
         nc.sync.dma_start(out=w1_rows[:], in_=W1.rearrange("(q u) n -> q u n", u=PACK))
+        b1_all = keep.tile([P, MID], BF16)
+        nc.sync.dma_start(out=b1_all[:], in_=b1.partition_broadcast(P))
 
         warm = keep.tile([P, 1], F32)
         nc.vector.memset(warm[:], 0.0)
@@ -115,11 +118,10 @@ def tile_samplequerymessagepassing_pa_s_kernel(
                 out=q_f32[half][:], in0=loaded[("qs", half)][:], in1=loaded[("pe", half)][:], op=ADD
             )
             nc.scalar.copy(out=x_bf[half][:, :, C:K0], in_=q_f32[half][:])
-            transpose_words(half, 1)
         for half in range(HALVES):
-            nc.vector.tensor_tensor(
-                out=x_bf[half][:, :, 0:C], in0=sf_all[:, half * HALF_GROUPS : (half + 1) * HALF_GROUPS, :], in1=q_f32[half][:], op=SUBTRACT
-            )
+            sf = sf_all[:, half * HALF_GROUPS : (half + 1) * HALF_GROUPS, :]
+            nc.vector.tensor_tensor(out=x_bf[half][:, :, 0:C], in0=sf, in1=q_f32[half][:], op=SUBTRACT)
+            transpose_words(half, 1)
             transpose_words(half, 0)
 
         def empty_words(half):
@@ -131,12 +133,23 @@ def tile_samplequerymessagepassing_pa_s_kernel(
                 in_=xt[half][:].rearrange("p g v r -> p g r v"),
             )
 
+        spare = psum.tile([P, MID], F32, tag="bank")
+        for half in range(HALVES):
+            sf = sf_all[:, half * HALF_GROUPS : (half + 1) * HALF_GROUPS, :]
+            nc.tensor.matmul(out=spare[:], lhsT=ones[:], rhs=sf.rearrange("p g c -> p (g c)"), start=True, stop=True)
+
         w0_grouped = keep.tile([P, PACK, P, PACK], BF16, align_bytes=64)
         w0_codes = keep.tile([P, MID], U32, align_bytes=64)
         w0_scales = keep.tile([P, MID], U8, align_bytes=64)
         x_codes = keep.tile([P, TOKENS], U32, align_bytes=64)
         x_scales = keep.tile([P, TOKENS], U8, align_bytes=64)
         w0_sorted = w0_rows[:].rearrange("p t (q u) -> p q t u", u=PACK)
+        w1_grouped = keep.tile([P, MID, PACK], BF16, align_bytes=64)
+        w1_codes = keep.tile([P, MID], U32, align_bytes=64)
+        w1_scales = keep.tile([P, MID], U8, align_bytes=64)
+        h_grouped = keep.tile([P, TOKENS, PACK], BF16, align_bytes=64)
+        h_codes = keep.tile([P, TOKENS], U32, align_bytes=64)
+        h_scales = keep.tile([P, TOKENS], U8, align_bytes=64)
 
         def quantise_x(half):
             quantise(
@@ -152,98 +165,83 @@ def tile_samplequerymessagepassing_pa_s_kernel(
                 w0_grouped[:, half * 2 : half * 2 + 2, :, :].rearrange("p u q t -> p (u q t)"),
             )
 
-        w1_grouped = keep.tile([P, MID, PACK], BF16, align_bytes=64)
-        w1_codes = keep.tile([P, MID], U32, align_bytes=64)
-        w1_scales = keep.tile([P, MID], U8, align_bytes=64)
-        h_grouped = keep.tile([P, TOKENS, PACK], BF16, align_bytes=64)
-        h_codes = keep.tile([P, TOKENS], U32, align_bytes=64)
-        h_scales = keep.tile([P, TOKENS], U8, align_bytes=64)
+        def regroup_w1(cols, copy=nc.vector.tensor_copy):
+            regroup(w1_grouped[:, cols, :], w1_rows[:, :, cols], copy)
 
         def quantise_w1(half):
-            quantise(
-                w1_codes[:, half_of(half)],
-                w1_scales[:, half_of(half)],
-                w1_grouped[:, half_of(half), :].rearrange("p c j -> p (c j)"),
-            )
+            cols = half_of(half)
+            quantise(w1_codes[:, cols], w1_scales[:, cols], w1_grouped[:, cols, :].rearrange("p c j -> p (c j)"))
 
-        def quantise_h(half):
-            quantise(
-                h_codes[:, half_of(half)],
-                h_scales[:, half_of(half)],
-                h_grouped[:, half_of(half), :].rearrange("p c u -> p (c u)"),
-            )
+        def quantise_h(g):
+            cols = group_of(g)
+            quantise(h_codes[:, cols], h_scales[:, cols], h_grouped[:, cols, :].rearrange("p c u -> p (c u)"))
 
         nc.scalar.copy(out=w0_grouped[:, 3, :, :], in_=w0_sorted[:, :, :, 3])
         empty_words(0)
         empty_words(1)
+        regroup_w1(group_of(3), nc.scalar.copy)
         nc.vector.tensor_copy(
             out=w0_grouped[:, 0:2, :, :].rearrange("p u q t -> p q t u"), in_=w0_sorted[:, :, :, 0:2]
         )
         nc.vector.tensor_copy(out=w0_grouped[:, 2, :, :], in_=w0_sorted[:, :, :, 2])
-        regroup(w1_grouped[:, half_of(0), :], w1_rows[:, :, half_of(0)])
         quantise_x(0)
         quantise_w0(0)
         quantise_w0(1)
         quantise_x(1)
-        regroup(w1_grouped[:, half_of(1), :], w1_rows[:, :, half_of(1)])
+        regroup_w1(half_of(0))
+        regroup_w1(group_of(2))
         quantise_w1(0)
-
-        spare = psum.tile([P, MID], F32, tag="bank")
-        for half in range(HALVES):
-            nc.tensor.matmul(
-                out=spare[:],
-                lhsT=ones[:],
-                rhs=sf_all[:, half * HALF_GROUPS : (half + 1) * HALF_GROUPS, :].rearrange("p g c -> p (g c)"),
-                start=True,
-                stop=True,
-            )
-
-        b1_ps = psum.tile([P, MID], F32, tag="bank")
-        nc.tensor.matmul(out=b1_ps[:], lhsT=ones[:], rhs=b1_row[:], start=True, stop=True)
-        b1_all = keep.tile([P, MID], F32)
+        quantise_w1(1)
 
         h_bf = []
         for half in range(HALVES):
             h_bf.append(keep.tile([P, PACK, HALF], BF16, name="h_bf%d" % half))
-
-        def layer1(half, pair):
-            h_ps = psum.tile([P, 2, HALF], F32, tag="bank", name="h_ps%d%d" % (half, pair))
-            for i in range(2):
-                u = 2 * pair + i
-                cols = slice(u * P, (u + 1) * P)
+            for u in range(PACK):
+                h_ps = psum.tile([P, HALF], F32, tag="bank", name="h_ps%d%d" % (half, u))
+                cols = group_of(u)
                 mx_pass(
-                    h_ps[:, i, :],
+                    h_ps[:],
                     (w0_codes[:, cols], w0_scales[:, cols]),
                     (x_codes[:, half_of(half)], x_scales[:, half_of(half)]),
                 )
-            for i in range(2):
-                u = 2 * pair + i
                 nc.scalar.activation(
-                    out=h_bf[half][:, u, :], in_=h_ps[:, i, :], func=GELU, bias=b0_bf[:, u : u + 1], scale=1.0
+                    out=h_bf[half][:, u, :], in_=h_ps[:], func=GELU, bias=b0_bf[:, u : u + 1], scale=1.0
                 )
 
-        layer1(0, 0)
-        layer1(0, 1)
-        layer1(1, 0)
-        layer1(1, 1)
-        nc.scalar.copy(out=b1_all[:], in_=b1_ps[:])
+        def regroup_h(g, copy=nc.vector.tensor_copy):
+            half, i = divmod(g, HALF_GROUPS)
+            regroup(h_grouped[:, group_of(g), :], h_bf[half][:, :, group_of(i)], copy)
+
+        o_ps = {}
 
         def layer2(g):
-            cols = slice(g * P, (g + 1) * P)
-            o_ps = psum.tile([P, MID], F32, tag="bank")
-            mx_pass(o_ps[:], (h_codes[:, cols], h_scales[:, cols]), (w1_codes[:], w1_scales[:]))
-            biased = keep.tile([P, MID], F32, name="biased%d" % g)
-            nc.vector.tensor_tensor(out=biased[:], in0=o_ps[:], in1=b1_all[:], op=ADD)
-            result = keep.tile([P, MID], F32, name="result%d" % g)
-            nc.scalar.activation(out=result[:], in_=biased[:], func=GELU)
-            nc.sync.dma_start(out=by_group(out)[:, g, :], in_=result[:])
+            cols = group_of(g)
+            o_ps[g] = psum.tile([P, MID], F32, tag="bank", name="o_ps%d" % g)
+            mx_pass(o_ps[g][:], (h_codes[:, cols], h_scales[:, cols]), (w1_codes[:], w1_scales[:]))
 
-        regroup(h_grouped[:, half_of(0), :], h_bf[0][:])
-        quantise_w1(1)
+        def finish(g, pieces):
+            width = MID // pieces
+            for i in range(pieces):
+                cols = slice(i * width, (i + 1) * width)
+                biased = keep.tile([P, width], F32, name="biased%d%d" % (g, i))
+                nc.vector.tensor_tensor(out=biased[:], in0=o_ps[g][:, cols], in1=b1_all[:, cols], op=ADD)
+                result = keep.tile([P, width], F32, name="result%d%d" % (g, i))
+                nc.scalar.activation(out=result[:], in_=biased[:], func=GELU)
+                nc.sync.dma_start(out=by_group(out)[:, g, cols], in_=result[:])
+
+        regroup_h(3, nc.scalar.copy)
+        regroup_h(0)
+        regroup_h(1)
         quantise_h(0)
-        regroup(h_grouped[:, half_of(1), :], h_bf[1][:])
         layer2(0)
         quantise_h(1)
         layer2(1)
+        regroup_h(2)
+        finish(0, 1)
+        quantise_h(2)
         layer2(2)
+        finish(1, 1)
+        quantise_h(3)
         layer2(3)
+        finish(2, 1)
+        finish(3, 2)

@@ -69,11 +69,11 @@ def tile_samplequerymessagepassing_pa_s_kernel(
         ctx.enter_context(tc.manual_schedule())
 
         loaded = {}
-        for half in range(HALVES):
-            groups = slice(half * HALF_GROUPS, (half + 1) * HALF_GROUPS)
+        chunks = [slice(0, 1), slice(1, 2), slice(2, 4)]
+        for i, groups in enumerate(chunks):
             for name, dram in (("qs", query_samples), ("pe", pos_enc)):
-                loaded[(name, half)] = keep.tile([P, HALF_GROUPS, C], BF16, name="%s%d" % (name, half))
-                nc.sync.dma_start(out=loaded[(name, half)][:], in_=by_group(dram)[:, groups, :])
+                loaded[(name, i)] = keep.tile([P, groups.stop - groups.start, C], BF16, name="%s%d" % (name, i))
+                nc.sync.dma_start(out=loaded[(name, i)][:], in_=by_group(dram)[:, groups, :])
         sf_all = keep.tile([P, GROUPS, C], BF16)
         nc.sync.dma_start(out=sf_all[:], in_=by_group(sample_features))
         w0_rows = keep.tile([P, PACK, MID], BF16)
@@ -114,9 +114,12 @@ def tile_samplequerymessagepassing_pa_s_kernel(
                 nc.tensor.transpose(xt[half][:, i, v, :], words[:, first : first + P], ident[:])
 
         for half in range(HALVES):
-            nc.vector.tensor_tensor(
-                out=q_f32[half][:], in0=loaded[("qs", half)][:], in1=loaded[("pe", half)][:], op=ADD
-            )
+            for i, groups in enumerate(chunks):
+                if groups.start // HALF_GROUPS == half:
+                    mine = slice(groups.start - half * HALF_GROUPS, groups.stop - half * HALF_GROUPS)
+                    nc.vector.tensor_tensor(
+                        out=q_f32[half][:, mine, :], in0=loaded[("qs", i)][:], in1=loaded[("pe", i)][:], op=ADD
+                    )
             nc.scalar.copy(out=x_bf[half][:, :, C:K0], in_=q_f32[half][:])
         for half in range(HALVES):
             sf = sf_all[:, half * HALF_GROUPS : (half + 1) * HALF_GROUPS, :]
@@ -184,11 +187,11 @@ def tile_samplequerymessagepassing_pa_s_kernel(
             out=w0_grouped[:, 0:2, :, :].rearrange("p u q t -> p q t u"), in_=w0_sorted[:, :, :, 0:2]
         )
         nc.vector.tensor_copy(out=w0_grouped[:, 2, :, :], in_=w0_sorted[:, :, :, 2])
-        quantise_x(0)
         quantise_w0(0)
+        quantise_x(0)
         quantise_w0(1)
-        quantise_x(1)
         regroup_w1(half_of(0))
+        quantise_x(1)
         regroup_w1(group_of(2))
         quantise_w1(0)
         quantise_w1(1)
@@ -240,8 +243,8 @@ def tile_samplequerymessagepassing_pa_s_kernel(
         finish(0, 1)
         quantise_h(2)
         layer2(2)
-        finish(1, 1)
         quantise_h(3)
         layer2(3)
+        finish(1, 1)
         finish(2, 1)
         finish(3, 2)

@@ -73,7 +73,8 @@ def tile_samplequerymessagepassing_pa_s_kernel(
         for i, groups in enumerate(chunks):
             for name, dram in (("qs", query_samples), ("pe", pos_enc)):
                 loaded[(name, i)] = keep.tile([P, groups.stop - groups.start, C], BF16, name="%s%d" % (name, i))
-                nc.sync.dma_start(out=loaded[(name, i)][:], in_=by_group(dram)[:, groups, :])
+                queue = nc.scalar if name == "pe" else nc.sync
+                queue.dma_start(out=loaded[(name, i)][:], in_=by_group(dram)[:, groups, :])
         sf_all = keep.tile([P, GROUPS, C], BF16)
         nc.sync.dma_start(out=sf_all[:], in_=by_group(sample_features))
         w0_rows = keep.tile([P, PACK, MID], BF16)
@@ -247,4 +248,4 @@ def tile_samplequerymessagepassing_pa_s_kernel(
         layer2(3)
         finish(1, 1)
         finish(2, 1)
-        finish(3, 2)
+        finish(3, 1)

@@ -180,14 +180,14 @@ def tile_samplequerymessagepassing_pa_s_kernel(
             cols = group_of(g)
             quantise(h_codes[:, cols], h_scales[:, cols], h_grouped[:, cols, :].rearrange("p c u -> p (c u)"))
 
-        nc.scalar.copy(out=w0_grouped[:, 3, :, :], in_=w0_sorted[:, :, :, 3])
         empty_words(0)
         empty_words(1)
         regroup_w1(group_of(3), nc.scalar.copy)
-        nc.vector.tensor_copy(
-            out=w0_grouped[:, 0:2, :, :].rearrange("p u q t -> p q t u"), in_=w0_sorted[:, :, :, 0:2]
-        )
-        nc.vector.tensor_copy(out=w0_grouped[:, 2, :, :], in_=w0_sorted[:, :, :, 2])
+        for pair in range(2):
+            passes = slice(2 * pair, 2 * pair + 2)
+            nc.vector.tensor_copy(
+                out=w0_grouped[:, passes, :, :].rearrange("p u q t -> p q t u"), in_=w0_sorted[:, :, :, passes]
+            )
         quantise_w0(0)
         quantise_x(0)
         quantise_w0(1)

@@ -81,10 +81,10 @@ def tile_samplequerymessagepassing_pa_s_kernel(
         nc.sync.dma_start(
             out=w0_rows[:].rearrange("p (v e) n -> p v e n", e=2), in_=W0.rearrange("(v p e) n -> p v e n", p=P, e=2)
         )
-        b0_bf = keep.tile([P, PACK], BF16)
-        nc.sync.dma_start(out=b0_bf[:], in_=b0.rearrange("(q u) -> q u", u=PACK))
         w1_rows = keep.tile([P, PACK, MID], BF16)
         nc.sync.dma_start(out=w1_rows[:], in_=W1.rearrange("(q u) n -> q u n", u=PACK))
+        b0_bf = keep.tile([P, PACK], BF16)
+        nc.sync.dma_start(out=b0_bf[:], in_=b0.rearrange("(q u) -> q u", u=PACK))
         b1_all = keep.tile([P, MID], BF16)
         nc.sync.dma_start(out=b1_all[:], in_=b1.partition_broadcast(P))
 
@@ -104,15 +104,25 @@ def tile_samplequerymessagepassing_pa_s_kernel(
         xt = []
         for half in range(HALVES):
             q_f32.append(keep.tile([P, HALF_GROUPS, C], F32, name="q_f32_%d" % half))
-            x_bf.append(keep.tile([P, HALF_GROUPS, K0], BF16, name="x_bf_%d" % half))
+            x_bf.append(
+                [
+                    keep.tile([P, HALF_GROUPS, C], BF16, name="d_bf_%d" % half),
+                    keep.tile([P, HALF_GROUPS, C], BF16, name="q_bf_%d" % half),
+                ]
+            )
             x_grouped.append(keep.tile([P, HALF_GROUPS, P, PACK], BF16, name="x_grouped%d" % half, align_bytes=64))
             xt.append(psum.tile([P, HALF_GROUPS, 2, P], F32, tag="bank", name="xt%d" % half))
 
         def transpose_words(half, v):
-            words = x_bf[half][:].rearrange("p g c -> p (g c)").bitcast(F32)
+            words = x_bf[half][v][:].rearrange("p g c -> p (g c)").bitcast(F32)
             for i in range(HALF_GROUPS):
-                first = i * C + v * P
-                nc.tensor.transpose(xt[half][:, i, v, :], words[:, first : first + P], ident[:])
+                nc.tensor.transpose(xt[half][:, i, v, :], words[:, group_of(i)], ident[:])
+
+        spare = psum.tile([P, C], F32, tag="bank")
+        for i in range(2):
+            for name in ("qs", "pe"):
+                rhs = loaded[(name, i)][:].rearrange("p g c -> p (g c)")
+                nc.tensor.matmul(out=spare[:], lhsT=ones[:], rhs=rhs, start=True, stop=True)
 
         for half in range(HALVES):
             for i, groups in enumerate(chunks):
@@ -121,10 +131,10 @@ def tile_samplequerymessagepassing_pa_s_kernel(
                     nc.vector.tensor_tensor(
                         out=q_f32[half][:, mine, :], in0=loaded[("qs", i)][:], in1=loaded[("pe", i)][:], op=ADD
                     )
-            nc.scalar.copy(out=x_bf[half][:, :, C:K0], in_=q_f32[half][:])
+            nc.scalar.copy(out=x_bf[half][1][:], in_=q_f32[half][:])
         for half in range(HALVES):
             sf = sf_all[:, half * HALF_GROUPS : (half + 1) * HALF_GROUPS, :]
-            nc.vector.tensor_tensor(out=x_bf[half][:, :, 0:C], in0=sf, in1=q_f32[half][:], op=SUBTRACT)
+            nc.vector.tensor_tensor(out=x_bf[half][0][:], in0=sf, in1=q_f32[half][:], op=SUBTRACT)
             transpose_words(half, 1)
             transpose_words(half, 0)
 
@@ -136,11 +146,6 @@ def tile_samplequerymessagepassing_pa_s_kernel(
                 .rearrange("p (g r v) -> p g r v", r=P, v=2),
                 in_=xt[half][:].rearrange("p g v r -> p g r v"),
             )
-
-        spare = psum.tile([P, MID], F32, tag="bank")
-        for half in range(HALVES):
-            sf = sf_all[:, half * HALF_GROUPS : (half + 1) * HALF_GROUPS, :]
-            nc.tensor.matmul(out=spare[:], lhsT=ones[:], rhs=sf.rearrange("p g c -> p (g c)"), start=True, stop=True)
 
         w0_grouped = keep.tile([P, PACK, P, PACK], BF16, align_bytes=64)
         w0_codes = keep.tile([P, MID], U32, align_bytes=64)

@@ -187,7 +187,6 @@ def tile_samplequerymessagepassing_pa_s_kernel(
 
         empty_words(0)
         empty_words(1)
-        regroup_w1(group_of(3), nc.scalar.copy)
         for pair in range(2):
             passes = slice(2 * pair, 2 * pair + 2)
             nc.vector.tensor_copy(
@@ -198,7 +197,7 @@ def tile_samplequerymessagepassing_pa_s_kernel(
         quantise_w0(1)
         regroup_w1(half_of(0))
         quantise_x(1)
-        regroup_w1(group_of(2))
+        regroup_w1(half_of(1))
         quantise_w1(0)
         quantise_w1(1)
 

from contextlib import ExitStack

import concourse.mybir as mybir
from concourse.masks import make_identity

BF16 = mybir.dt.bfloat16
F32 = mybir.dt.float32
U32 = mybir.dt.uint32
U8 = mybir.dt.uint8
FP8X4 = mybir.dt.float8_e4m3fn_x4
GELU = mybir.ActivationFunctionType.Gelu_apprx_tanh
ADD = mybir.AluOpType.add
SUBTRACT = mybir.AluOpType.subtract

P = 128
PACK = 4
TOKENS = 512
C = 256
K0 = 2 * C
MID = 512
GROUPS = TOKENS // P
HALVES = 2
HALF_GROUPS = GROUPS // HALVES
HALF = TOKENS // HALVES
RUN = 4

FLOPS = 2 * TOKENS * K0 * MID + 2 * TOKENS * MID * MID


def group_of(index):
    return slice(index * P, (index + 1) * P)


def half_of(index):
    return slice(index * HALF, (index + 1) * HALF)


def tile_samplequerymessagepassing_pa_s_kernel(
    tc, sample_features, query_samples, pos_enc, W0, b0, W1, b1, out
):
    nc = tc.nc

    def by_group(dram):
        return dram.flatten_outer_dims().rearrange("(r g) c -> r g c", g=GROUPS)

    def regroup(grouped, rows, copy=nc.vector.tensor_copy):
        copy(
            out=grouped.rearrange("p (c i) j -> p c j i", i=RUN),
            in_=rows.rearrange("p j (c i) -> p c j i", i=RUN),
        )

    def quantise(codes, scales, grouped):
        nc.vector.quantize_mx(out=codes.bitcast(FP8X4), scales=scales, in_=grouped)

    def mx_pass(acc, stationary, moving):
        nc.tensor.matmul_mx(
            out=acc,
            lhsT=stationary[0].bitcast(FP8X4),
            lhsT_scale=stationary[1],
            rhs=moving[0].bitcast(FP8X4),
            rhs_scale=moving[1],
            start=True,
            stop=True,
        )

    with ExitStack() as ctx:
        keep = ctx.enter_context(tc.tile_pool(name="keep", bufs=1))
        psum = ctx.enter_context(tc.psum_pool(name="psum", bufs=8))
        ctx.enter_context(tc.manual_schedule())

        loaded = {}
        chunks = [slice(0, 1), slice(1, 2), slice(2, 4)]
        for i, groups in enumerate(chunks):
            for name, dram in (("qs", query_samples), ("pe", pos_enc)):
                loaded[(name, i)] = keep.tile([P, groups.stop - groups.start, C], BF16, name="%s%d" % (name, i))
                queue = nc.scalar if name == "pe" else nc.sync
                queue.dma_start(out=loaded[(name, i)][:], in_=by_group(dram)[:, groups, :])
        sf_all = keep.tile([P, GROUPS, C], BF16)
        nc.sync.dma_start(out=sf_all[:], in_=by_group(sample_features))
        w0_rows = keep.tile([P, PACK, MID], BF16)
        nc.sync.dma_start(
            out=w0_rows[:].rearrange("p (v e) n -> p v e n", e=2), in_=W0.rearrange("(v p e) n -> p v e n", p=P, e=2)
        )
        w1_rows = keep.tile([P, PACK, MID], BF16)
        nc.sync.dma_start(out=w1_rows[:], in_=W1.rearrange("(q u) n -> q u n", u=PACK))
        b0_bf = keep.tile([P, PACK], BF16)
        nc.sync.dma_start(out=b0_bf[:], in_=b0.rearrange("(q u) -> q u", u=PACK))
        b1_all = keep.tile([P, MID], BF16)
        nc.sync.dma_start(out=b1_all[:], in_=b1.partition_broadcast(P))

        warm = keep.tile([P, 1], F32)
        nc.vector.memset(warm[:], 0.0)
        warmed = keep.tile([P, 1], F32)
        nc.scalar.activation(out=warmed[:], in_=warm[:], func=GELU)

        ident = keep.tile([P, P], F32)
        make_identity(nc, ident[:])
        ones = keep.tile([P, P], BF16)
        nc.gpsimd.memset(ones[:], 1.0)

        q_f32 = []
        x_bf = []
        x_grouped = []
        xt = []
        for half in range(HALVES):
            q_f32.append(keep.tile([P, HALF_GROUPS, C], F32, name="q_f32_%d" % half))
            x_bf.append(
                [
                    keep.tile([P, HALF_GROUPS, C], BF16, name="d_bf_%d" % half),
                    keep.tile([P, HALF_GROUPS, C], BF16, name="q_bf_%d" % half),
                ]
            )
            x_grouped.append(keep.tile([P, HALF_GROUPS, P, PACK], BF16, name="x_grouped%d" % half, align_bytes=64))
            xt.append(psum.tile([P, HALF_GROUPS, 2, P], F32, tag="bank", name="xt%d" % half))

        def transpose_words(half, v):
            words = x_bf[half][v][:].rearrange("p g c -> p (g c)").bitcast(F32)
            for i in range(HALF_GROUPS):
                nc.tensor.transpose(xt[half][:, i, v, :], words[:, group_of(i)], ident[:])

        spare = psum.tile([P, C], F32, tag="bank")
        for i in range(2):
            for name in ("qs", "pe"):
                rhs = loaded[(name, i)][:].rearrange("p g c -> p (g c)")
                nc.tensor.matmul(out=spare[:], lhsT=ones[:], rhs=rhs, start=True, stop=True)

        for half in range(HALVES):
            for i, groups in enumerate(chunks):
                if groups.start // HALF_GROUPS == half:
                    mine = slice(groups.start - half * HALF_GROUPS, groups.stop - half * HALF_GROUPS)
                    nc.vector.tensor_tensor(
                        out=q_f32[half][:, mine, :], in0=loaded[("qs", i)][:], in1=loaded[("pe", i)][:], op=ADD
                    )
            nc.scalar.copy(out=x_bf[half][1][:], in_=q_f32[half][:])
        for half in range(HALVES):
            sf = sf_all[:, half * HALF_GROUPS : (half + 1) * HALF_GROUPS, :]
            nc.vector.tensor_tensor(out=x_bf[half][0][:], in0=sf, in1=q_f32[half][:], op=SUBTRACT)
            transpose_words(half, 1)
            transpose_words(half, 0)

        def empty_words(half):
            nc.scalar.copy(
                out=x_grouped[half][:]
                .rearrange("p g r t -> p (g r t)")
                .bitcast(F32)
                .rearrange("p (g r v) -> p g r v", r=P, v=2),
                in_=xt[half][:].rearrange("p g v r -> p g r v"),
            )

        w0_grouped = keep.tile([P, PACK, P, PACK], BF16, align_bytes=64)
        w0_codes = keep.tile([P, MID], U32, align_bytes=64)
        w0_scales = keep.tile([P, MID], U8, align_bytes=64)
        x_codes = keep.tile([P, TOKENS], U32, align_bytes=64)
        x_scales = keep.tile([P, TOKENS], U8, align_bytes=64)
        w0_sorted = w0_rows[:].rearrange("p t (q u) -> p q t u", u=PACK)
        w1_grouped = keep.tile([P, MID, PACK], BF16, align_bytes=64)
        w1_codes = keep.tile([P, MID], U32, align_bytes=64)
        w1_scales = keep.tile([P, MID], U8, align_bytes=64)
        h_grouped = keep.tile([P, TOKENS, PACK], BF16, align_bytes=64)
        h_codes = keep.tile([P, TOKENS], U32, align_bytes=64)
        h_scales = keep.tile([P, TOKENS], U8, align_bytes=64)

        def quantise_x(half):
            quantise(
                x_codes[:, half_of(half)],
                x_scales[:, half_of(half)],
                x_grouped[half][:].rearrange("p g r t -> p (g r t)"),
            )

        def quantise_w0(half):
            quantise(
                w0_codes[:, half_of(half)],
                w0_scales[:, half_of(half)],
                w0_grouped[:, half * 2 : half * 2 + 2, :, :].rearrange("p u q t -> p (u q t)"),
            )

        def regroup_w1(cols, copy=nc.vector.tensor_copy):
            regroup(w1_grouped[:, cols, :], w1_rows[:, :, cols], copy)

        def quantise_w1(half):
            cols = half_of(half)
            quantise(w1_codes[:, cols], w1_scales[:, cols], w1_grouped[:, cols, :].rearrange("p c j -> p (c j)"))

        def quantise_h(g):
            cols = group_of(g)
            quantise(h_codes[:, cols], h_scales[:, cols], h_grouped[:, cols, :].rearrange("p c u -> p (c u)"))

        empty_words(0)
        empty_words(1)
        for pair in range(2):
            passes = slice(2 * pair, 2 * pair + 2)
            nc.vector.tensor_copy(
                out=w0_grouped[:, passes, :, :].rearrange("p u q t -> p q t u"), in_=w0_sorted[:, :, :, passes]
            )
        quantise_w0(0)
        quantise_x(0)
        quantise_w0(1)
        regroup_w1(half_of(0))
        quantise_x(1)
        regroup_w1(half_of(1))
        quantise_w1(0)
        quantise_w1(1)

        h_bf = []
        for half in range(HALVES):
            h_bf.append(keep.tile([P, PACK, HALF], BF16, name="h_bf%d" % half))
            for u in range(PACK):
                h_ps = psum.tile([P, HALF], F32, tag="bank", name="h_ps%d%d" % (half, u))
                cols = group_of(u)
                mx_pass(
                    h_ps[:],
                    (w0_codes[:, cols], w0_scales[:, cols]),
                    (x_codes[:, half_of(half)], x_scales[:, half_of(half)]),
                )
                nc.scalar.activation(
                    out=h_bf[half][:, u, :], in_=h_ps[:], func=GELU, bias=b0_bf[:, u : u + 1], scale=1.0
                )

        def regroup_h(g, copy=nc.vector.tensor_copy):
            half, i = divmod(g, HALF_GROUPS)
            regroup(h_grouped[:, group_of(g), :], h_bf[half][:, :, group_of(i)], copy)

        o_ps = {}

        def layer2(g):
            cols = group_of(g)
            o_ps[g] = psum.tile([P, MID], F32, tag="bank", name="o_ps%d" % g)
            mx_pass(o_ps[g][:], (h_codes[:, cols], h_scales[:, cols]), (w1_codes[:], w1_scales[:]))

        def finish(g, pieces):
            width = MID // pieces
            for i in range(pieces):
                cols = slice(i * width, (i + 1) * width)
                biased = keep.tile([P, width], F32, name="biased%d%d" % (g, i))
                nc.vector.tensor_tensor(out=biased[:], in0=o_ps[g][:, cols], in1=b1_all[:, cols], op=ADD)
                result = keep.tile([P, width], F32, name="result%d%d" % (g, i))
                nc.scalar.activation(out=result[:], in_=biased[:], func=GELU)
                nc.sync.dma_start(out=by_group(out)[:, g, cols], in_=result[:])

        regroup_h(3, nc.scalar.copy)
        regroup_h(0)
        regroup_h(1)
        quantise_h(0)
        layer2(0)
        quantise_h(1)
        layer2(1)
        regroup_h(2)
        finish(0, 1)
        quantise_h(2)
        layer2(2)
        quantise_h(3)
        layer2(3)
        finish(1, 1)
        finish(2, 1)
        finish(3, 1)
